import numpy as np
import ml_dtypes


def mxq(x, axis, fmt="e4m3"):
    dtype, down = {"e4m3": (ml_dtypes.float8_e4m3fn, 7), "e5m2": (ml_dtypes.float8_e5m2, 14)}[fmt]
    v = np.moveaxis(np.asarray(x, np.float32).astype(ml_dtypes.bfloat16).astype(np.float64), axis, -1)
    blocks = v.reshape(v.shape[:-1] + (-1, 32))
    amax = np.abs(blocks).max(-1, keepdims=True)
    byte = np.maximum(np.where(amax > 0, np.frexp(amax)[1] - 1 + 127, 0) - down, 1)
    scale = np.exp2(byte - 127.0)
    codes = (blocks / scale).astype(np.float32).astype(dtype).astype(np.float64)
    return np.moveaxis((codes * scale).reshape(v.shape), -1, axis)


WIDE = False


def mx_kscale(k):
    if not WIDE:
        return np.ones(k)
    levels = np.array([10, -10, 5, -5, 0])
    if k % 512:
        return np.exp2(np.random.permutation(np.resize(levels, k // 32))).repeat(32)
    a = np.empty((k // 512, 16))
    for p in range(k // 512):
        a[p, :8] = np.random.permutation(np.resize(levels, 8))
        for g in range(8):
            far = levels[np.abs(levels - a[p, g]) >= 10]
            a[p, g + 8] = far[np.random.randint(len(far))]
    return np.exp2(a.ravel()).repeat(32)


BF16 = ml_dtypes.bfloat16


def bf(x):
    return np.asarray(x, np.float32).astype(BF16)


def f64(x):
    return np.asarray(x).astype(np.float64)


B, N, ATTR, STATE, REL, G, NF = 4, 32, 4, 16, 9, 32, 1024


def draw0():
    rn = np.random.standard_normal
    s, u, t = mx_kscale(NF), mx_kscale(NF), mx_kscale(NF)
    rp_rows = np.concatenate([s, u, u])
    pp_rows = np.concatenate([u, t])
    pp_scale = np.concatenate([np.full(NF, 1.0 / np.sqrt(NF)), np.full(NF, 1.0 / np.sqrt(NF * N))])
    return {
        "rel_enc": bf(np.maximum(rn((B, N, N, NF)) * 1.1, 0.0) * s),
        "obj": bf(np.maximum(rn((B, N, NF)) * 1.1, 0.0) * u),
        "rp_w": bf(rn((3 * NF, NF)) * 2.0 / np.sqrt(3 * NF * N) / rp_rows[:, None] * t),
        "rp_b": bf(rn(NF) * 0.1 * t),
        "pp_w": bf(rn((2 * NF, NF)) * (pp_scale / pp_rows)[:, None]),
        "pp_b": bf(rn(NF) * 0.1),
    }


def core(rel_enc, obj, rp_w, rp_b, pp_w, pp_b):
    rp, pp = f64(rp_w), f64(pp_w)
    oq = mxq(f64(obj), 2, "e4m3")
    e_rel = mxq(f64(rel_enc), 3, "e4m3") @ mxq(rp[:NF], 0, "e4m3")
    e_recv = oq @ mxq(rp[NF:2 * NF], 0, "e4m3")
    e_send = oq @ mxq(rp[2 * NF:], 0, "e4m3")
    rel_eff = np.maximum(e_rel + e_recv[:, :, None, :] + e_send[:, None, :, :] + f64(rp_b), 0.0)
    agg = rel_eff.sum(axis=2)
    p_obj = oq @ mxq(pp[:NF], 0, "e4m3")
    p_agg = mxq(agg, 2, "e4m3") @ mxq(pp[NF:], 0, "e4m3")
    return np.maximum(p_obj + p_agg + f64(pp_b), 0.0)


def e4m3fn_bytes(y):
    return np.clip(np.asarray(y, np.float64), -448.0, 448.0).astype(np.float32).astype(ml_dtypes.float8_e4m3fn).view(np.uint8)


def e4m3fn_values(b):
    return np.asarray(b, np.uint8).view(ml_dtypes.float8_e4m3fn).astype(np.float64)


def setup_inputs():
    d = draw0()
    x0 = np.asarray(d['rel_enc']).astype(np.float64)
    s = (np.max(np.abs(x0), axis=(0, 1, 2), keepdims=True) / 448.0).astype(np.float32)
    out = {}
    for k, v in d.items():
        if k == 'rel_enc':
            out['rel_enc_bytes'] = e4m3fn_bytes(x0 / s.astype(np.float64))
            out['rel_enc_scale'] = s
        else:
            out[k] = v
    return out


def reference(rel_enc_bytes, rel_enc_scale, obj, rp_w, rp_b, pp_w, pp_b):
    return core(e4m3fn_values(rel_enc_bytes) * rel_enc_scale.astype(np.float64), obj, rp_w, rp_b, pp_w, pp_b)

from contextlib import ExitStack

import concourse.mybir as mybir
from concourse.masks import make_identity

P = 128
NF = 1024
K_PASS = 512
PASSES = NF // K_PASS
GRAPHS = 4
N = 32
GROUP = 256
GROUPS = GRAPHS * N * N // GROUP
RECV_PER_GROUP = GROUP // N

F32 = mybir.dt.float32
BF16 = mybir.dt.bfloat16
U32 = mybir.dt.uint32
I32 = mybir.dt.int32
U8 = mybir.dt.uint8
FP8 = mybir.dt.float8_e4m3fn
FP8X4 = mybir.dt.float8_e4m3fn_x4
ALU = mybir.AluOpType
ACT = mybir.ActivationFunctionType

FLOPS = 2 * GRAPHS * N * N * NF * NF + 4 * 2 * GRAPHS * N * NF * NF


def tile_compositionalkoopmanoperators_pa_kernel(
    tc, rel_bytes, rel_scale, obj, rp_w, rp_b, pp_w, pp_b, out
):
    nc = tc.nc
    rel_rows = rel_bytes.rearrange("b i j k -> (b i j) k").rearrange("(g p t) k -> g p (t k)", p=P, t=2)
    obj_rows = obj.rearrange("b n k -> (b n) k").rearrange("(x t) k -> t x k", t=2)
    out_rows = out.rearrange("b n k -> (b n) k").rearrange("(x t) k -> t x k", t=2)

    with ExitStack() as ctx:
        keep = ctx.enter_context(tc.tile_pool(name="keep", bufs=1))
        loads = ctx.enter_context(tc.tile_pool(name="loads", bufs=6))
        work = ctx.enter_context(tc.tile_pool(name="work", bufs=3))
        psum = ctx.enter_context(tc.psum_pool(name="psum", bufs=2))

        def kept(shape, dtype, name):
            return keep.tile(shape, dtype, name=name, tag=name, align_bytes=64)

        ident = kept([P, P], F32, "ident")
        make_identity(nc, ident[:])

        ctx.enter_context(tc.manual_schedule())

        sc8 = kept([P, NF // P], F32, "sc8")
        nc.scalar.dma_start(out=sc8[:], in_=rel_scale.rearrange("a b c (p e) -> p (a b c e)", p=P))
        ob = kept([P, NF], BF16, "ob")
        for t in range(2):
            nc.scalar.dma_start(out=ob[64 * t : 64 * t + 64, :], in_=obj_rows[t])
        rpb = kept([P, 2, 4], BF16, "rpb")
        with nc.allow_non_contiguous_dma(reason="bias"):
            nc.scalar.dma_start(out=rpb[:], in_=rp_b.rearrange("(q p t) -> p q t", p=P, t=4))

        raws = {}
        rel_raw = {}

        def load_rel(g):
            rb = loads.tile([P, 2 * NF], U8, name="rb", tag="rb", align_bytes=64)
            nc.sync.dma_start(out=rb[:], in_=rel_rows[g])
            rel_raw[g] = rb

        def load_w(key, w, row, g, q):
            raw = loads.tile([P, 4, 512], BF16, name="raw", tag="raw", bufs=12, align_bytes=64)
            r0 = row + K_PASS * g
            nc.sync.dma_start(
                out=raw[:],
                in_=w[r0 : r0 + K_PASS, 512 * q : 512 * q + 512].rearrange("(p j) n -> p j n", j=4),
            )
            raws[key, g, q] = raw

        rp_rows = {"r": 0, "i": NF, "s": 2 * NF}

        load_rel(0)
        for key in ("r", "s", "i"):
            for g in range(PASSES):
                load_w(key, rp_w, rp_rows[key], g, 0)
        for g in range(1, 4):
            load_rel(g)
        for key in ("r", "s", "i"):
            for g in range(PASSES):
                load_w(key, rp_w, rp_rows[key], g, 1)

        scale = kept([P, NF], F32, "scale")
        scale_v = scale[:].rearrange("m (p e) -> m e p", e=8)
        for half in range(2):
            bank = psum.tile([P, 4, P], F32, name="misc", tag="misc")
            for e in range(4):
                c = 4 * half + e
                nc.tensor.transpose(bank[:, e, :], sc8[:, c : c + 1].to_broadcast([P, P]), ident[:])
            nc.scalar.copy(out=scale_v[:, 4 * half : 4 * half + 4, :], in_=bank[:])

        og = kept([P, PASSES * P * 4], BF16, "og")
        bank = psum.tile([P, 4, P], F32, name="misc", tag="misc")
        words = ob[:].bitcast(F32)
        for g in range(PASSES):
            for u in range(2):
                nc.tensor.transpose(bank[:, 2 * g + u, :], words[:, 256 * g + u : 256 * g + 256 : 2], ident[:])
        nc.scalar.copy(
            out=og[:].bitcast(F32).rearrange("p (g r u) -> p g r u", g=2, u=2),
            in_=bank[:].rearrange("p (g u) r -> p g r u", g=2),
        )
        oc = kept([P, PASSES * P], U32, "oc")
        osc = kept([P, PASSES * P], U8, "osc")
        nc.gpsimd.memset(osc[:].bitcast(I32), 0)

        codes = {}
        scales = {}
        rbias = {}
        repc = {}
        reps = {}

        def weight_ig(key, g, q, h, engine):
            wg = work.tile([P, 1024], BF16, name="wg", tag="wg", bufs=4, align_bytes=64)
            engine(
                out=wg[:].rearrange("p (t m j) -> p t m j", t=2, j=4),
                in_=raws[key, g, q][:].rearrange("p j (m t) -> p t m j", t=4)[:, 2 * h : 2 * h + 2],
            )
            return wg

        def weight_q(key, g, q, h, wg):
            name = "w%s%d%d%d" % (key, g, q, h)
            c = kept([P, 256], U32, name + "c")
            s = kept([P, 256], U8, name + "s")
            nc.vector.quantize_mx(out=c[:].bitcast(FP8X4), scales=s[:], in_=wg[:])
            codes[key, g, q, h] = c
            scales[key, g, q, h] = s

        def weights(q, h):
            first = q == 0 and h == 0
            order = [(key, g) for key in ("r", "s", "i") for g in range(PASSES)]
            pending = []
            for key, g in order:
                eng = nc.scalar.copy if first and key == "s" else nc.vector.tensor_copy
                pending.append((key, g, weight_ig(key, g, q, h, eng)))
                if len(pending) > 2:
                    k0, g0, w0 = pending.pop(0)
                    weight_q(k0, g0, q, h, w0)
            for k0, g0, w0 in pending:
                weight_q(k0, g0, q, h, w0)

        def receivers(q, h):
            bank = psum.tile([P, 2, P], F32, name="misc", tag="misc")
            for n in range(2):
                for g in range(PASSES):
                    nc.tensor.matmul_mx(
                        out=bank[:, n, :],
                        lhsT=codes["i", g, q, h][:, 128 * n : 128 * n + 128].bitcast(FP8X4),
                        lhsT_scale=scales["i", g, q, h][:, 128 * n : 128 * n + 128],
                        rhs=oc[:, P * g : P * g + P].bitcast(FP8X4),
                        rhs_scale=osc[:, P * g : P * g + P],
                        start=(g == 0),
                        stop=(g == PASSES - 1),
                    )
            rb = kept([P, 2, P], F32, "rbias%d%d" % (q, h))
            for n in range(2):
                t = 2 * h + n
                nc.scalar.activation(rb[:, n, :], bank[:, n, :], ACT.Identity, bias=rpb[:, q, t : t + 1])
            rbias[q, h] = rb

        def replicate(b):
            c = work.tile([P, PASSES * GROUP], U32, name="repc", tag="repc", bufs=4, align_bytes=64)
            s = work.tile([P, PASSES * GROUP], U8, name="reps", tag="reps", bufs=4, align_bytes=64)
            for dst, src, w in ((c, oc, 16), (s, osc, 4)):
                for g in range(PASSES):
                    nc.vector.tensor_copy(
                        out=dst[:].bitcast(I32).rearrange("p (g t i w) -> p g t i w", g=2, t=2, i=8)[:, g],
                        in_=src[:].bitcast(I32).rearrange("p (g t b w) -> p g t b w", g=2, t=2, b=4)[:, g, :, b, :]
                        .unsqueeze(2)
                        .to_broadcast([P, 2, 8, w]),
                    )
            repc[b] = c
            reps[b] = s

        wide = {}
        turned = {}
        grouped = {}
        rel_codes = {}
        rel_scales = {}

        def widen(g):
            for t in range(2):
                wb = work.tile([P, NF], BF16, name="wb", tag="wb", bufs=4, align_bytes=64)
                nc.vector.tensor_tensor(
                    out=wb[:], in0=rel_raw[g][:, NF * t : NF * t + NF].bitcast(FP8), in1=scale[:], op=ALU.mult
                )
                wide[g, t] = wb

        def turn(g):
            for t in range(2):
                bank = psum.tile([P, 4, P], F32, name="tr", tag="tr")
                words = wide[g, t][:].bitcast(F32)
                for kp in range(PASSES):
                    for u in range(2):
                        nc.tensor.transpose(
                            bank[:, 2 * kp + u, :], words[:, 256 * kp + u : 256 * kp + 256 : 2], ident[:]
                        )
                turned[g, t] = bank

        def empty(g):
            grp = work.tile([P, PASSES * GROUP * 4], BF16, name="grp", tag="grp", align_bytes=64)
            view = grp[:].bitcast(F32).rearrange("p (g t r u) -> p g t r u", g=2, t=2, u=2)
            for t in range(2):
                nc.scalar.copy(out=view[:, :, t], in_=turned[g, t][:].rearrange("p (g u) r -> p g r u", g=2))
            grouped[g] = grp

        def quantise(g):
            c = kept([P, PASSES * GROUP], U32, "rc%d" % g)
            s = kept([P, PASSES * GROUP], U8, "rs%d" % g)
            nc.vector.quantize_mx(out=c[:].bitcast(FP8X4), scales=s[:], in_=grouped[g][:])
            rel_codes[g] = c
            rel_scales[g] = s

        agg = [kept([P, 4, P], F32, "agg%d" % q) for q in range(2)]

        def unit(g, q, h):
            b = g // 4
            bank = psum.tile([P, 2, GROUP], F32, name="acc", tag="acc", bufs=4)
            for n in range(2):
                cols = slice(128 * n, 128 * n + 128)
                for i, (key, mc, ms) in enumerate((("s", repc[b], reps[b]), ("r", rel_codes[g], rel_scales[g]))):
                    for kp in range(PASSES):
                        nc.tensor.matmul_mx(
                            out=bank[:, n, :],
                            lhsT=codes[key, kp, q, h][:, cols].bitcast(FP8X4),
                            lhsT_scale=scales[key, kp, q, h][:, cols],
                            rhs=mc[:, GROUP * kp : GROUP * kp + GROUP].bitcast(FP8X4),
                            rhs_scale=ms[:, GROUP * kp : GROUP * kp + GROUP],
                            start=(i == 0 and kp == 0),
                            stop=(i == 1 and kp == PASSES - 1),
                        )
            junk = work.tile([P, 2, RECV_PER_GROUP, N], BF16, name="junk", tag="junk", bufs=4)
            for n in range(2):
                view = bank[:, n, :].rearrange("p (t i w) -> p i t w", t=2, i=RECV_PER_GROUP)
                for il in range(RECV_PER_GROUP):
                    i = RECV_PER_GROUP * (g % 4) + il
                    col = 64 * (i % 2) + 16 * b + i // 2
                    nc.scalar.activation(
                        junk[:, n, il, :].rearrange("p (t w) -> p t w", t=2),
                        view[:, il],
                        ACT.Relu,
                        bias=rbias[q, h][:, n, col : col + 1],
                        accum_out=agg[q][:, 2 * h + n, col : col + 1],
                    )

        sets = [(0, 0), (0, 1), (1, 0), (1, 1)]
        tasks = [("r", 0), ("w", 0), ("r", 1), ("w", 1), ("r", 2), ("r", 3), ("w", 2), ("r", 4), ("r", 5), ("w", 3)]
        tasks += [("r", g) for g in range(6, GROUPS)]
        tasks += [("o", n) for n in range(8)]
        cost = {"r": 2.2, "w": 4.6, "o": 1.6}
        unit_cost = 1.05

        late = [("g", g) for g in range(4, GROUPS)]
        late += [("o", key, row, g, q) for key, row in (("o", 0), ("a", NF)) for g in range(PASSES) for q in range(2)]
        late_n = 0

        ready_groups = []
        ready_sets = []
        queue = []
        budget = 0.0
        fresh_group = None
        last_rel = None

        for kind, n in tasks + [("end", 0), ("end", 1)]:
            new_units = []
            for item in late[late_n : late_n + 2]:
                if item[0] == "g":
                    load_rel(item[1])
                else:
                    load_w(item[1], pp_w, item[2], item[3], item[4])
            late_n += 2
            if kind == "r":
                widen(n)
            elif kind == "w":
                q, h = sets[n]
                if n == 0:
                    nc.vector.quantize_mx(out=oc[:].bitcast(FP8X4), scales=osc[:], in_=og[:])
                weights(q, h)
            elif kind == "o":
                key, g, q = ("o", "a")[n // 4], (n // 2) % 2, n % 2
                wg = work.tile([P, 512, 4], BF16, name="og4", tag="og4", bufs=2, align_bytes=64)
                nc.vector.tensor_copy(out=wg[:], in_=raws[key, g, q][:].rearrange("p j n -> p n j"))
                c = kept([P, 512], U32, "w%s%d%dc" % (key, g, q))
                s = kept([P, 512], U8, "w%s%d%ds" % (key, g, q))
                nc.vector.quantize_mx(
                    out=c[:].bitcast(FP8X4), scales=s[:], in_=wg[:].rearrange("p n j -> p (n j)")
                )
                codes[key, g, q] = c
                scales[key, g, q] = s
            if last_rel is not None:
                empty(last_rel)
                if last_rel % 4 == 0:
                    replicate(last_rel // 4)
                quantise(last_rel)
                new_units += [(last_rel, s) for s in ready_sets]
                ready_groups.append(last_rel)
                last_rel = None
            if kind == "w":
                receivers(q, h)
                new_units += [(g, (q, h)) for g in ready_groups]
                ready_sets.append((q, h))
            budget = min(budget + cost.get(kind, 1000.0), 1000.0)
            while queue and budget >= unit_cost:
                g, s = queue.pop(0)
                unit(g, s[0], s[1])
                budget -= unit_cost
            if not queue:
                budget = 0.0
            queue += new_units
            if kind == "r":
                turn(n)
                last_rel = n

        pb = kept([P, NF], BF16, "pb")
        nc.sync.dma_start(out=pb[:], in_=pp_b.partition_broadcast(P))
        ac = []
        asc = []
        for q in range(2):
            ag = work.tile([P, P, 4], BF16, name="ag", tag="ag", bufs=2, align_bytes=64)
            nc.vector.tensor_copy(out=ag[:], in_=agg[q][:].rearrange("p t c -> p c t"))
            c = kept([P, P], U32, "ac%d" % q)
            s = kept([P, P], U8, "as%d" % q)
            nc.vector.quantize_mx(out=c[:].bitcast(FP8X4), scales=s[:], in_=ag[:].rearrange("p c t -> p (c t)"))
            ac.append(c)
            asc.append(s)
        for h in range(2):
            bank = psum.tile([P, 512], F32, name="misc", tag="misc")
            terms = [("o", g, oc[:, P * g : P * g + P], osc[:, P * g : P * g + P]) for g in range(PASSES)]
            terms += [("a", g, ac[g][:], asc[g][:]) for g in range(PASSES)]
            for i, (key, g, lc, ls) in enumerate(terms):
                nc.tensor.matmul_mx(
                    out=bank[:],
                    lhsT=lc.bitcast(FP8X4),
                    lhsT_scale=ls,
                    rhs=codes[key, g, h][:].bitcast(FP8X4),
                    rhs_scale=scales[key, g, h][:],
                    start=(i == 0),
                    stop=(i == 3),
                )
            o1 = work.tile([P, 512], F32, name="o1", tag="o1", bufs=2)
            nc.vector.tensor_tensor(out=o1[:], in0=bank[:], in1=pb[:, 512 * h : 512 * h + 512], op=ALU.add)
            o2 = work.tile([P, 512], F32, name="o2", tag="o2", bufs=2)
            nc.scalar.activation(o2[:], o1[:], ACT.Relu)
            for t in range(2):
                nc.sync.dma_start(out=out_rows[t][:, 512 * h : 512 * h + 512], in_=o2[64 * t : 64 * t + 64, :])
